import numpy as np
import ml_dtypes


def mxq(x, axis, fmt="e4m3"):
    dtype, down = {"e4m3": (ml_dtypes.float8_e4m3fn, 7), "e5m2": (ml_dtypes.float8_e5m2, 14)}[fmt]
    v = np.moveaxis(np.asarray(x, np.float32).astype(ml_dtypes.bfloat16).astype(np.float64), axis, -1)
    blocks = v.reshape(v.shape[:-1] + (-1, 32))
    amax = np.abs(blocks).max(-1, keepdims=True)
    byte = np.maximum(np.where(amax > 0, np.frexp(amax)[1] - 1 + 127, 0) - down, 1)
    scale = np.exp2(byte - 127.0)
    codes = (blocks / scale).astype(np.float32).astype(dtype).astype(np.float64)
    return np.moveaxis((codes * scale).reshape(v.shape), -1, axis)


WIDE = False


def mx_kscale(k):
    if not WIDE:
        return np.ones(k)
    levels = np.array([10, -10, 5, -5, 0])
    a = np.random.permutation(np.resize(levels, k // 512 * 4)).reshape(k // 512, 4)
    idx = np.arange(k)
    return np.exp2(a[idx // 512, idx % 128 // 32])


BF16 = ml_dtypes.bfloat16


def bf(x):
    return np.asarray(x, np.float32).astype(BF16)


def f64(x):
    return np.asarray(x).astype(np.float64)


B, CIN, P, COUT, W, H, HEADS = 8, 1024, 512, 2048, 16, 32, 4
D = P // HEADS
N = W * H
EPS = 1e-5


def setup_inputs():
    s = mx_kscale(P)
    rel_h = np.random.standard_normal((HEADS, D, 1, H)) * 0.25
    rel_w = np.random.standard_normal((HEADS, D, W, 1)) * 0.25
    return {
        "h1": bf(np.maximum(np.random.standard_normal((B, P, N)), 0.0) * s[None, :, None]),
        "v_w": bf(np.random.standard_normal((P, P)) * 1.5 / np.sqrt(P) / s[None, :]),
        "v_b": bf(np.random.standard_normal(P) * 0.3),
        "q": bf(np.random.standard_normal((B, P, N)) * 0.35),
        "k": bf(np.random.standard_normal((B, P, N)) * 0.35),
        "pos": bf((rel_h + rel_w).reshape(HEADS, D, N)),
        "bn2_g": bf(np.random.uniform(0.5, 1.5, P)),
        "bn2_b": bf(np.random.standard_normal(P) * 0.3),
        "bn2_m": bf(np.random.standard_normal(P) * 0.3),
        "bn2_v": bf(np.random.uniform(0.5, 1.5, P)),
    }


def reference(h1, v_w, v_b, q, k, pos, bn2_g, bn2_b, bn2_m, bn2_v):
    v = (mxq(f64(v_w), 1, "e4m3") @ mxq(f64(h1), 1, "e4m3")) + f64(v_b)[None, :, None]
    q4 = f64(q).reshape(B, HEADS, D, N)
    k4 = f64(k).reshape(B, HEADS, D, N)
    s = q4.transpose(0, 1, 3, 2) @ k4 + f64(pos).transpose(0, 2, 1) @ q4
    e = np.exp(s - s.max(-1, keepdims=True))
    o = mxq(v.reshape(B, HEADS, D, N), 3, "e4m3") @ mxq(e, 3, "e4m3").transpose(0, 1, 3, 2)
    o = (o / e.sum(-1)[:, :, None, :]).reshape(B, P, N)
    scale = f64(bn2_g) / np.sqrt(f64(bn2_v) + EPS)
    y = (o - f64(bn2_m)[None, :, None]) * scale[None, :, None] + f64(bn2_b)[None, :, None]
    return np.maximum(y, 0.0)

@@ -1,0 +1,323 @@
+from contextlib import ExitStack
+
+import concourse.mybir as mybir
+from concourse.masks import make_identity
+
+BF16 = mybir.dt.bfloat16
+F32 = mybir.dt.float32
+U32 = mybir.dt.uint32
+U8 = mybir.dt.uint8
+FP8X4 = mybir.dt.float8_e4m3fn_x4
+ACT = mybir.ActivationFunctionType
+ALU = mybir.AluOpType
+AXIS = mybir.AxisListType
+
+P = 128
+PACK = 4
+BATCH = 8
+HEADS = 4
+CHANNELS = HEADS * P
+POSITIONS = PACK * P
+TILES = POSITIONS // P
+PAIRS = BATCH * HEADS
+WEIGHTS = -1
+EPS = 1e-5
+
+FLOPS = 2 * (BATCH * CHANNELS * CHANNELS * POSITIONS + 3 * PAIRS * P * POSITIONS * POSITIONS)
+
+
+def tile_bottleneck_transformer_pa_t_kernel(
+    tc, h1, v_w, v_b, q, k, pos, bn2_g, bn2_b, bn2_m, bn2_v, out
+):
+    nc = tc.nc
+    with ExitStack() as ctx:
+        keep = ctx.enter_context(tc.tile_pool(name="keep", bufs=1))
+        work = ctx.enter_context(tc.tile_pool(name="work", bufs=2))
+        psum = ctx.enter_context(tc.psum_pool(name="psum", bufs=1))
+        ctx.enter_context(tc.manual_schedule())
+
+        bn_rows = keep.tile([P, P], BF16)
+        nc.vector.memset(bn_rows[:], 0.0)
+        for r, vec in enumerate((bn2_g, bn2_b, bn2_m, bn2_v)):
+            nc.scalar.dma_start(
+                out=bn_rows[r * HEADS : (r + 1) * HEADS, :], in_=vec.rearrange("(h d) -> h d", h=HEADS)
+            )
+        vb_all = keep.tile([P, CHANNELS], BF16)
+        nc.scalar.dma_start(out=vb_all[:], in_=v_b.partition_broadcast(P))
+
+        q_sb, k_sb, h_sb = [], [], []
+        for b in range(BATCH):
+            q_sb.append(keep.tile([P, HEADS, POSITIONS], BF16, name="q%d" % b))
+            k_sb.append(keep.tile([P, HEADS, POSITIONS], BF16, name="k%d" % b))
+            h_sb.append(keep.tile([P, PACK, POSITIONS], BF16, name="h%d" % b))
+        pos_sb = keep.tile([P, HEADS, POSITIONS], BF16)
+        w_sb = keep.tile([P, TILES, CHANNELS], BF16)
+
+        def load_batch(b):
+            nc.sync.dma_start(out=q_sb[b][:], in_=q[b].rearrange("(h d) n -> d h n", h=HEADS))
+            nc.sync.dma_start(out=k_sb[b][:], in_=k[b].rearrange("(h d) n -> d h n", h=HEADS))
+            if b == 0:
+                nc.sync.dma_start(out=pos_sb[:], in_=pos.rearrange("h d n -> d h n"))
+                nc.sync.dma_start(out=w_sb[:], in_=v_w.rearrange("(c p) i -> p c i", p=P))
+            nc.sync.dma_start(out=h_sb[b][:], in_=h1[b].rearrange("(t p) m -> p t m", p=P))
+
+        for b in range(BATCH):
+            load_batch(b)
+
+        ident_bf = keep.tile([P, P], BF16)
+        make_identity(nc, ident_bf[:])
+        ident_f32 = keep.tile([P, P], F32)
+        make_identity(nc, ident_f32[:])
+
+        bn_flipped = psum.tile([P, P], BF16, tag="back", bufs=1)
+        nc.tensor.transpose(out=bn_flipped[:], in_=bn_rows[:], identity=ident_bf[:])
+        bn_cols = keep.tile([P, 4 * HEADS], F32)
+        nc.vector.tensor_copy(out=bn_cols[:], in_=bn_flipped[:, 0 : 4 * HEADS])
+        gain = bn_cols[:, 0 * HEADS : 1 * HEADS]
+        shift = bn_cols[:, 1 * HEADS : 2 * HEADS]
+        mean = bn_cols[:, 2 * HEADS : 3 * HEADS]
+        variance = bn_cols[:, 3 * HEADS : 4 * HEADS]
+        bn_std = keep.tile([P, HEADS], F32)
+        nc.vector.tensor_scalar_add(out=bn_std[:], in0=variance, scalar1=EPS)
+        nc.scalar.activation(out=bn_std[:], in_=bn_std[:], func=ACT.Sqrt)
+        bn_scale = keep.tile([P, HEADS], F32)
+        nc.vector.reciprocal(out=bn_scale[:], in_=bn_std[:])
+        nc.vector.tensor_mul(out=bn_scale[:], in0=bn_scale[:], in1=gain)
+        bn_shift = keep.tile([P, HEADS], F32)
+        nc.vector.tensor_mul(out=bn_shift[:], in0=mean, in1=bn_scale[:])
+        nc.vector.tensor_sub(out=bn_shift[:], in0=shift, in1=bn_shift[:])
+
+        rows = {WEIGHTS: w_sb}
+        row_sum = {}
+        flipped = {}
+        grouped = {}
+        codes, scales = {}, {}
+        h_grouped, h_codes, h_scales = {}, {}, {}
+        v_bank, v_grouped, v_codes, v_scales = {}, {}, {}, {}
+        o_bank, o_rows, o_back = {}, {}, {}
+
+        def is_pair(j):
+            return 0 <= j < PAIRS
+
+        def scores_and_flips(i, nt):
+            n_cols = slice(nt * P, (nt + 1) * P)
+            if is_pair(i):
+                b, h = divmod(i, HEADS)
+                s_bank = psum.tile([P, POSITIONS], F32, tag="scores", bufs=3)
+                nc.tensor.matmul(
+                    out=s_bank[:], lhsT=q_sb[b][:, h, n_cols], rhs=k_sb[b][:, h, :], start=True, stop=False
+                )
+            flip(i - 1, nt, 0)
+            flip(i - 1, nt, 1)
+            if is_pair(i):
+                nc.tensor.matmul(
+                    out=s_bank[:], lhsT=pos_sb[:, h, n_cols], rhs=q_sb[b][:, h, :], start=False, stop=True
+                )
+            flip(i - 1, nt, 2)
+            flip(i - 1, nt, 3)
+            if is_pair(i):
+                if nt == 0:
+                    e_rows = work.tile([P, TILES, POSITIONS], BF16, bufs=3)
+                    rows[i] = e_rows
+                    e_sum = work.tile([P, TILES], F32, bufs=4)
+                    row_sum[i] = e_sum
+                neg_max = work.tile([P, 1], F32, bufs=4)
+                nc.vector.tensor_reduce(out=neg_max[:], in_=s_bank[:], axis=AXIS.X, op=ALU.max, negate=True)
+                nc.scalar.activation(
+                    out=rows[i][:, nt, :],
+                    in_=s_bank[:],
+                    func=ACT.Exp,
+                    bias=neg_max[:],
+                    scale=1.0,
+                    accum_out=row_sum[i][:, nt : nt + 1],
+                )
+
+        def flip(j, nt, t):
+            if not (j == WEIGHTS or is_pair(j)):
+                return
+            half, a = divmod(nt, 2)
+            if a == 0 and t == 0:
+                flip_bank = psum.tile([P, 2, PACK, P], BF16, tag="flipped", bufs=2)
+                flipped[(j, half)] = flip_bank
+            nc.tensor.transpose(
+                out=flipped[(j, half)][:, a, t, :], in_=rows[j][:, nt, t * P : (t + 1) * P], identity=ident_bf[:]
+            )
+
+        def group_rows(j, half):
+            if not (j == WEIGHTS or is_pair(j)):
+                return
+            side_by_side = work.tile([P, 2, P, PACK], BF16, bufs=4, align_bytes=64)
+            grouped[(j, half)] = side_by_side
+            nc.scalar.copy(out=side_by_side[:], in_=flipped[(j, half)][:].rearrange("p a t r -> p a r t"))
+
+        def quantise_rows(j, half):
+            if not (j == WEIGHTS or is_pair(j)):
+                return
+            if j == WEIGHTS:
+                words = keep.tile([P, 2 * P], U32, name="w_words%d" % half, align_bytes=64)
+                plane = keep.tile([P, 2 * P], U8, name="w_plane%d" % half, align_bytes=64)
+            else:
+                words = work.tile([P, 2 * P], U32, bufs=4, align_bytes=64)
+                plane = work.tile([P, 2 * P], U8, bufs=4, align_bytes=64)
+            codes[(j, half)] = words
+            scales[(j, half)] = plane
+            nc.vector.quantize_mx(
+                out=words[:].bitcast(FP8X4),
+                scales=plane[:],
+                in_=grouped[(j, half)][:].rearrange("p a r t -> p (a r t)"),
+            )
+
+        def row_tile_operand(j, nt):
+            half, a = divmod(nt, 2)
+            cols = slice(a * P, (a + 1) * P)
+            return codes[(j, half)][:, cols].bitcast(FP8X4), scales[(j, half)][:, cols]
+
+        def group_h1(b, mt):
+            if not 0 <= b < BATCH:
+                return
+            h_side = work.tile([P, P, PACK], BF16, bufs=4, align_bytes=64)
+            h_grouped[(b, mt)] = h_side
+            nc.vector.tensor_copy(
+                out=h_side[:].rearrange("p (c i) t -> p c t i", i=4),
+                in_=h_sb[b][:, :, mt * P : (mt + 1) * P].rearrange("p t (c i) -> p c t i", i=4),
+            )
+
+        def quantise_h1(b, mt):
+            if not 0 <= b < BATCH:
+                return
+            if mt == 0:
+                h_words = work.tile([P, POSITIONS], U32, bufs=3, align_bytes=64)
+                h_plane = work.tile([P, POSITIONS], U8, bufs=3, align_bytes=64)
+                h_codes[b] = h_words
+                h_scales[b] = h_plane
+            m_cols = slice(mt * P, (mt + 1) * P)
+            nc.vector.quantize_mx(
+                out=h_codes[b][:, m_cols].bitcast(FP8X4),
+                scales=h_scales[b][:, m_cols],
+                in_=h_grouped[(b, mt)][:].rearrange("p m t -> p (m t)"),
+            )
+
+        def project_v(j):
+            if not is_pair(j):
+                return
+            b, h = divmod(j, HEADS)
+            vt_bank = psum.tile([P, TILES, P], F32, tag="mx", bufs=2)
+            v_bank[j] = vt_bank
+            w_words, w_plane = row_tile_operand(WEIGHTS, h)
+            for mt in range(TILES):
+                m_cols = slice(mt * P, (mt + 1) * P)
+                nc.tensor.matmul_mx(
+                    out=vt_bank[:, mt, :],
+                    lhsT=h_codes[b][:, m_cols].bitcast(FP8X4),
+                    lhsT_scale=h_scales[b][:, m_cols],
+                    rhs=w_words,
+                    rhs_scale=w_plane,
+                    start=True,
+                    stop=True,
+                )
+
+        def bias_v(j):
+            if not is_pair(j):
+                return
+            h = j % HEADS
+            v_side = work.tile([P, P, PACK], BF16, bufs=2, align_bytes=64)
+            v_grouped[j] = v_side
+            nc.vector.tensor_tensor(
+                out=v_side[:],
+                in0=v_bank[j][:].rearrange("p t d -> p d t"),
+                in1=vb_all[:, h * P : (h + 1) * P].unsqueeze(2).to_broadcast([P, P, PACK]),
+                op=ALU.add,
+            )
+
+        def quantise_v(j):
+            if not is_pair(j):
+                return
+            v_words = work.tile([P, P], U32, bufs=3, align_bytes=64)
+            v_plane = work.tile([P, P], U8, bufs=3, align_bytes=64)
+            v_codes[j] = v_words
+            v_scales[j] = v_plane
+            nc.vector.quantize_mx(
+                out=v_words[:].bitcast(FP8X4), scales=v_plane[:], in_=v_grouped[j][:].rearrange("p d t -> p (d t)")
+            )
+
+        def attend(j):
+            if not is_pair(j):
+                return
+            ot_bank = psum.tile([P, TILES, P], F32, tag="mx", bufs=2)
+            o_bank[j] = ot_bank
+            for nt in range(TILES):
+                e_words, e_plane = row_tile_operand(j, nt)
+                nc.tensor.matmul_mx(
+                    out=ot_bank[:, nt, :],
+                    lhsT=e_words,
+                    lhsT_scale=e_plane,
+                    rhs=v_codes[j][:].bitcast(FP8X4),
+                    rhs_scale=v_scales[j][:],
+                    start=True,
+                    stop=True,
+                )
+
+        def normalise(j):
+            if not is_pair(j):
+                return
+            inv_sum = work.tile([P, TILES], F32, bufs=2)
+            nc.vector.reciprocal(out=inv_sum[:], in_=row_sum[j][:])
+            ot_rows = work.tile([P, TILES, P], F32, bufs=2)
+            o_rows[j] = ot_rows
+            nc.vector.tensor_tensor(
+                out=ot_rows[:],
+                in0=o_bank[j][:],
+                in1=inv_sum[:].unsqueeze(2).to_broadcast([P, TILES, P]),
+                op=ALU.mult,
+            )
+
+        def flip_back(j):
+            if not is_pair(j):
+                return
+            back_bank = psum.tile([P, POSITIONS], F32, tag="back", bufs=1)
+            o_back[j] = back_bank
+            for nt in range(TILES):
+                nc.tensor.transpose(
+                    out=back_bank[:, nt * P : (nt + 1) * P], in_=o_rows[j][:, nt, :], identity=ident_f32[:]
+                )
+
+        def finish(j):
+            if not is_pair(j):
+                return
+            b, h = divmod(j, HEADS)
+            y = work.tile([P, POSITIONS], F32, bufs=4)
+            nc.scalar.activation(
+                out=y[:], in_=o_back[j][:], func=ACT.Relu, bias=bn_shift[:, h : h + 1], scale=bn_scale[:, h : h + 1]
+            )
+            nc.sync.dma_start(out=out[b, h * P : (h + 1) * P, :], in_=y[:])
+
+        for i in range(PAIRS + 3):
+            h_batch, h_tile = divmod(i - 1, TILES)
+            h_batch = h_batch + 1 if i >= 1 else BATCH
+
+            scores_and_flips(i, 0)
+            finish(i - 3)
+            quantise_rows(i - 2, 1)
+            group_h1(h_batch, h_tile)
+
+            scores_and_flips(i, 1)
+            group_rows(i - 1, 0)
+            attend(i - 2)
+            project_v(i - 1)
+            quantise_h1(h_batch, h_tile)
+
+            scores_and_flips(i, 2)
+            normalise(i - 2)
+
+            scores_and_flips(i, 3)
+            group_rows(i - 1, 1)
+            bias_v(i - 1)
+            quantise_rows(i - 1, 0)
+            quantise_v(i - 1)
+            flip_back(i - 2)
+
+            if i == 0:
+                for mt in range(TILES):
+                    group_h1(0, mt)
+                for mt in range(TILES):
+                    quantise_h1(0, mt)

@@ -36,15 +36,6 @@ def tile_bottleneck_transformer_pa_t_kernel(
         psum = ctx.enter_context(tc.psum_pool(name="psum", bufs=1))
         ctx.enter_context(tc.manual_schedule())
 
-        bn_rows = keep.tile([P, P], BF16)
-        nc.vector.memset(bn_rows[:], 0.0)
-        for r, vec in enumerate((bn2_g, bn2_b, bn2_m, bn2_v)):
-            nc.scalar.dma_start(
-                out=bn_rows[r * HEADS : (r + 1) * HEADS, :], in_=vec.rearrange("(h d) -> h d", h=HEADS)
-            )
-        vb_all = keep.tile([P, CHANNELS], BF16)
-        nc.scalar.dma_start(out=vb_all[:], in_=v_b.partition_broadcast(P))
-
         q_sb, k_sb, h_sb = [], [], []
         for b in range(BATCH):
             q_sb.append(keep.tile([P, HEADS, POSITIONS], BF16, name="q%d" % b))
@@ -52,17 +43,33 @@ def tile_bottleneck_transformer_pa_t_kernel(
             h_sb.append(keep.tile([P, PACK, POSITIONS], BF16, name="h%d" % b))
         pos_sb = keep.tile([P, HEADS, POSITIONS], BF16)
         w_sb = keep.tile([P, TILES, CHANNELS], BF16)
+        bn_rows = keep.tile([P, P], BF16)
+        vb_all = keep.tile([P, CHANNELS], BF16)
 
-        def load_batch(b):
-            nc.sync.dma_start(out=q_sb[b][:], in_=q[b].rearrange("(h d) n -> d h n", h=HEADS))
-            nc.sync.dma_start(out=k_sb[b][:], in_=k[b].rearrange("(h d) n -> d h n", h=HEADS))
-            if b == 0:
-                nc.sync.dma_start(out=pos_sb[:], in_=pos.rearrange("h d n -> d h n"))
-                nc.sync.dma_start(out=w_sb[:], in_=v_w.rearrange("(c p) i -> p c i", p=P))
+        def load_first_batch_head(h):
+            d_rows = slice(h * P, (h + 1) * P)
+            nc.sync.dma_start(out=q_sb[0][:, h, :], in_=q[0, d_rows, :])
+            nc.sync.dma_start(out=k_sb[0][:, h, :], in_=k[0, d_rows, :])
+            nc.sync.dma_start(out=pos_sb[:, h, :], in_=pos[h])
+
+        def load_h1(b):
             nc.sync.dma_start(out=h_sb[b][:], in_=h1[b].rearrange("(t p) m -> p t m", p=P))
 
-        for b in range(BATCH):
-            load_batch(b)
+        load_first_batch_head(0)
+        nc.sync.dma_start(out=w_sb[:], in_=v_w.rearrange("(c p) i -> p c i", p=P))
+        nc.vector.memset(bn_rows[:], 0.0)
+        for r, vec in enumerate((bn2_g, bn2_b, bn2_m, bn2_v)):
+            nc.scalar.dma_start(
+                out=bn_rows[r * HEADS : (r + 1) * HEADS, :], in_=vec.rearrange("(h d) -> h d", h=HEADS)
+            )
+        nc.scalar.dma_start(out=vb_all[:], in_=v_b.partition_broadcast(P))
+        for h in range(1, HEADS):
+            load_first_batch_head(h)
+        load_h1(0)
+        for b in range(1, BATCH):
+            nc.sync.dma_start(out=q_sb[b][:], in_=q[b].rearrange("(h d) n -> d h n", h=HEADS))
+            nc.sync.dma_start(out=k_sb[b][:], in_=k[b].rearrange("(h d) n -> d h n", h=HEADS))
+            load_h1(b)
 
         ident_bf = keep.tile([P, P], BF16)
         make_identity(nc, ident_bf[:])
@@ -87,6 +94,7 @@ def tile_bottleneck_transformer_pa_t_kernel(
         nc.vector.tensor_mul(out=bn_shift[:], in0=mean, in1=bn_scale[:])
         nc.vector.tensor_sub(out=bn_shift[:], in0=shift, in1=bn_shift[:])
 
+        s_banks = {}
         rows = {WEIGHTS: w_sb}
         row_sum = {}
         flipped = {}
@@ -99,59 +107,66 @@ def tile_bottleneck_transformer_pa_t_kernel(
         def is_pair(j):
             return 0 <= j < PAIRS
 
-        def scores_and_flips(i, nt):
-            n_cols = slice(nt * P, (nt + 1) * P)
+        def has_rows(j):
+            return j == WEIGHTS or is_pair(j)
+
+        def scores(i, nt):
             if is_pair(i):
                 b, h = divmod(i, HEADS)
+                n_cols = slice(nt * P, (nt + 1) * P)
                 s_bank = psum.tile([P, POSITIONS], F32, tag="scores", bufs=3)
+                s_banks[(i, nt)] = s_bank
                 nc.tensor.matmul(
                     out=s_bank[:], lhsT=q_sb[b][:, h, n_cols], rhs=k_sb[b][:, h, :], start=True, stop=False
                 )
-            flip(i - 1, nt, 0)
-            flip(i - 1, nt, 1)
-            if is_pair(i):
                 nc.tensor.matmul(
                     out=s_bank[:], lhsT=pos_sb[:, h, n_cols], rhs=q_sb[b][:, h, :], start=False, stop=True
                 )
-            flip(i - 1, nt, 2)
-            flip(i - 1, nt, 3)
-            if is_pair(i):
-                if nt == 0:
-                    e_rows = work.tile([P, TILES, POSITIONS], BF16, bufs=3)
-                    rows[i] = e_rows
-                    e_sum = work.tile([P, TILES], F32, bufs=4)
-                    row_sum[i] = e_sum
-                neg_max = work.tile([P, 1], F32, bufs=4)
-                nc.vector.tensor_reduce(out=neg_max[:], in_=s_bank[:], axis=AXIS.X, op=ALU.max, negate=True)
-                nc.scalar.activation(
-                    out=rows[i][:, nt, :],
-                    in_=s_bank[:],
-                    func=ACT.Exp,
-                    bias=neg_max[:],
-                    scale=1.0,
-                    accum_out=row_sum[i][:, nt : nt + 1],
-                )
+            if has_rows(i - 1):
+                flip(i - 1, nt)
 
-        def flip(j, nt, t):
-            if not (j == WEIGHTS or is_pair(j)):
+        def softmax(i, nt):
+            if not is_pair(i):
                 return
-            half, a = divmod(nt, 2)
-            if a == 0 and t == 0:
-                flip_bank = psum.tile([P, 2, PACK, P], BF16, tag="flipped", bufs=2)
-                flipped[(j, half)] = flip_bank
-            nc.tensor.transpose(
-                out=flipped[(j, half)][:, a, t, :], in_=rows[j][:, nt, t * P : (t + 1) * P], identity=ident_bf[:]
+            if nt == 0:
+                e_rows = work.tile([P, TILES, POSITIONS], BF16, bufs=3)
+                rows[i] = e_rows
+                e_sum = work.tile([P, TILES], F32, bufs=4)
+                row_sum[i] = e_sum
+            neg_max = work.tile([P, 1], F32, bufs=4)
+            nc.vector.tensor_reduce(out=neg_max[:], in_=s_banks[(i, nt)][:], axis=AXIS.X, op=ALU.max, negate=True)
+            nc.scalar.activation(
+                out=rows[i][:, nt, :],
+                in_=s_banks[(i, nt)][:],
+                func=ACT.Exp,
+                bias=neg_max[:],
+                scale=1.0,
+                accum_out=row_sum[i][:, nt : nt + 1],
             )
 
+        def flip(j, nt):
+            half, a = divmod(nt, 2)
+            if a == 0:
+                flip_bank = psum.tile([P, 2, PACK, P], BF16, tag="flipped", bufs=2)
+                flipped[(j, half)] = flip_bank
+            for t in range(PACK):
+                nc.tensor.transpose(
+                    out=flipped[(j, half)][:, a, t, :], in_=rows[j][:, nt, t * P : (t + 1) * P], identity=ident_bf[:]
+                )
+
         def group_rows(j, half):
-            if not (j == WEIGHTS or is_pair(j)):
+            if not has_rows(j):
                 return
             side_by_side = work.tile([P, 2, P, PACK], BF16, bufs=4, align_bytes=64)
             grouped[(j, half)] = side_by_side
-            nc.scalar.copy(out=side_by_side[:], in_=flipped[(j, half)][:].rearrange("p a t r -> p a r t"))
+            alternately = flipped[(j, half)][:].rearrange("p a t r -> p a r t")
+            if half == 0:
+                nc.scalar.copy(out=side_by_side[:], in_=alternately)
+            else:
+                nc.vector.tensor_copy(out=side_by_side[:], in_=alternately)
 
         def quantise_rows(j, half):
-            if not (j == WEIGHTS or is_pair(j)):
+            if not has_rows(j):
                 return
             if j == WEIGHTS:
                 words = keep.tile([P, 2 * P], U32, name="w_words%d" % half, align_bytes=64)
@@ -172,19 +187,25 @@ def tile_bottleneck_transformer_pa_t_kernel(
             cols = slice(a * P, (a + 1) * P)
             return codes[(j, half)][:, cols].bitcast(FP8X4), scales[(j, half)][:, cols]
 
-        def group_h1(b, mt):
-            if not 0 <= b < BATCH:
+        def group_h1(g):
+            if not 0 <= g < BATCH * TILES:
                 return
-            h_side = work.tile([P, P, PACK], BF16, bufs=4, align_bytes=64)
-            h_grouped[(b, mt)] = h_side
-            nc.vector.tensor_copy(
+            b, mt = divmod(g, TILES)
+            h_side = work.tile([P, P, PACK], BF16, bufs=6, align_bytes=64)
+            h_grouped[g] = h_side
+            nc.gpsimd.tensor_scalar(
                 out=h_side[:].rearrange("p (c i) t -> p c t i", i=4),
-                in_=h_sb[b][:, :, mt * P : (mt + 1) * P].rearrange("p t (c i) -> p c t i", i=4),
+                in0=h_sb[b][:, :, mt * P : (mt + 1) * P].rearrange("p t (c i) -> p c t i", i=4),
+                scalar1=1.0,
+                scalar2=0.0,
+                op0=ALU.mult,
+                op1=ALU.add,
             )
 
-        def quantise_h1(b, mt):
-            if not 0 <= b < BATCH:
+        def quantise_h1(g):
+            if not 0 <= g < BATCH * TILES:
                 return
+            b, mt = divmod(g, TILES)
             if mt == 0:
                 h_words = work.tile([P, POSITIONS], U32, bufs=3, align_bytes=64)
                 h_plane = work.tile([P, POSITIONS], U8, bufs=3, align_bytes=64)
@@ -194,7 +215,7 @@ def tile_bottleneck_transformer_pa_t_kernel(
             nc.vector.quantize_mx(
                 out=h_codes[b][:, m_cols].bitcast(FP8X4),
                 scales=h_scales[b][:, m_cols],
-                in_=h_grouped[(b, mt)][:].rearrange("p m t -> p (m t)"),
+                in_=h_grouped[g][:].rearrange("p m t -> p (m t)"),
             )
 
         def project_v(j):
@@ -264,12 +285,10 @@ def tile_bottleneck_transformer_pa_t_kernel(
             nc.vector.reciprocal(out=inv_sum[:], in_=row_sum[j][:])
             ot_rows = work.tile([P, TILES, P], F32, bufs=2)
             o_rows[j] = ot_rows
-            nc.vector.tensor_tensor(
-                out=ot_rows[:],
-                in0=o_bank[j][:],
-                in1=inv_sum[:].unsqueeze(2).to_broadcast([P, TILES, P]),
-                op=ALU.mult,
-            )
+            for nt in range(TILES):
+                nc.scalar.activation(
+                    out=ot_rows[:, nt, :], in_=o_bank[j][:, nt, :], func=ACT.Copy, scale=inv_sum[:, nt : nt + 1]
+                )
 
         def flip_back(j):
             if not is_pair(j):
@@ -291,33 +310,34 @@ def tile_bottleneck_transformer_pa_t_kernel(
             )
             nc.sync.dma_start(out=out[b, h * P : (h + 1) * P, :], in_=y[:])
 
+        for g in range(TILES):
+            group_h1(g)
         for i in range(PAIRS + 3):
-            h_batch, h_tile = divmod(i - 1, TILES)
-            h_batch = h_batch + 1 if i >= 1 else BATCH
+            scores(i, 0)
+            group_rows(i - 2, 1)
+            softmax(i, 0)
+            group_h1(i + TILES)
 
-            scores_and_flips(i, 0)
-            finish(i - 3)
-            quantise_rows(i - 2, 1)
-            group_h1(h_batch, h_tile)
-
-            scores_and_flips(i, 1)
+            scores(i, 1)
+            quantise_rows(i - 2, 0)
+            bias_v(i - 2)
+            softmax(i, 1)
             group_rows(i - 1, 0)
+
+            scores(i, 2)
+            flip_back(i - 3)
+            quantise_rows(i - 2, 1)
+            quantise_v(i - 2)
+            softmax(i, 2)
+            finish(i - 3)
+
+            scores(i, 3)
             attend(i - 2)
             project_v(i - 1)
-            quantise_h1(h_batch, h_tile)
-
-            scores_and_flips(i, 2)
+            if i > 0:
+                quantise_h1(i + TILES - 1)
+            softmax(i, 3)
             normalise(i - 2)
-
-            scores_and_flips(i, 3)
-            group_rows(i - 1, 1)
-            bias_v(i - 1)
-            quantise_rows(i - 1, 0)
-            quantise_v(i - 1)
-            flip_back(i - 2)
-
             if i == 0:
-                for mt in range(TILES):
-                    group_h1(0, mt)
-                for mt in range(TILES):
-                    quantise_h1(0, mt)
+                for g in range(TILES):
+                    quantise_h1(g)

@@ -34,7 +34,6 @@ def tile_bottleneck_transformer_pa_t_kernel(
         keep = ctx.enter_context(tc.tile_pool(name="keep", bufs=1))
         work = ctx.enter_context(tc.tile_pool(name="work", bufs=2))
         psum = ctx.enter_context(tc.psum_pool(name="psum", bufs=1))
-        ctx.enter_context(tc.manual_schedule())
 
         q_sb, k_sb, h_sb = [], [], []
         for b in range(BATCH):

@@ -52,7 +52,11 @@ def tile_bottleneck_transformer_pa_t_kernel(
             nc.sync.dma_start(out=pos_sb[:, h, :], in_=pos[h])
 
         def load_h1(b):
-            nc.sync.dma_start(out=h_sb[b][:], in_=h1[b].rearrange("(t p) m -> p t m", p=P))
+            for u in range(2):
+                nc.sync.dma_start(
+                    out=h_sb[b][:, 2 * u : 2 * u + 2, :],
+                    in_=h1[b, 2 * P * u : 2 * P * (u + 1), :].rearrange("(p e) m -> p e m", e=2),
+                )
 
         load_first_batch_head(0)
         nc.sync.dma_start(out=w_sb[:], in_=v_w.rearrange("(c p) i -> p c i", p=P))
@@ -146,11 +150,12 @@ def tile_bottleneck_transformer_pa_t_kernel(
         def flip(j, nt):
             half, a = divmod(nt, 2)
             if a == 0:
-                flip_bank = psum.tile([P, 2, PACK, P], BF16, tag="flipped", bufs=2)
+                flip_bank = psum.tile([P, 2, 2, P], F32, tag="flipped", bufs=2)
                 flipped[(j, half)] = flip_bank
-            for t in range(PACK):
+            words = rows[j][:, nt, :].bitcast(F32)
+            for u in range(2):
                 nc.tensor.transpose(
-                    out=flipped[(j, half)][:, a, t, :], in_=rows[j][:, nt, t * P : (t + 1) * P], identity=ident_bf[:]
+                    out=flipped[(j, half)][:, a, u, :], in_=words[:, u * P : (u + 1) * P], identity=ident_f32[:]
                 )
 
         def group_rows(j, half):
@@ -158,11 +163,13 @@ def tile_bottleneck_transformer_pa_t_kernel(
                 return
             side_by_side = work.tile([P, 2, P, PACK], BF16, bufs=4, align_bytes=64)
             grouped[(j, half)] = side_by_side
-            alternately = flipped[(j, half)][:].rearrange("p a t r -> p a r t")
+            alternately = flipped[(j, half)][:].rearrange("p a u r -> p a r u")
+            as_words = side_by_side[:].rearrange("p a r t -> p (a r t)").bitcast(F32)
+            as_words = as_words.rearrange("p (a r u) -> p a r u", a=2, u=2)
             if half == 0:
-                nc.scalar.copy(out=side_by_side[:], in_=alternately)
+                nc.scalar.copy(out=as_words, in_=alternately)
             else:
-                nc.vector.tensor_copy(out=side_by_side[:], in_=alternately)
+                nc.vector.tensor_copy(out=as_words, in_=alternately)
 
         def quantise_rows(j, half):
             if not has_rows(j):
@@ -194,7 +201,9 @@ def tile_bottleneck_transformer_pa_t_kernel(
             h_grouped[g] = h_side
             nc.gpsimd.tensor_scalar(
                 out=h_side[:].rearrange("p (c i) t -> p c t i", i=4),
-                in0=h_sb[b][:, :, mt * P : (mt + 1) * P].rearrange("p t (c i) -> p c t i", i=4),
+                in0=h_sb[b][:, :, 2 * P * (mt // 2) + mt % 2 : 2 * P * (mt // 2 + 1) : 2].rearrange(
+                    "p t (c i) -> p c t i", i=4
+                ),
                 scalar1=1.0,
                 scalar2=0.0,
                 op0=ALU.mult,

@@ -87,15 +87,18 @@ def tile_bottleneck_transformer_pa_t_kernel(
         shift = bn_cols[:, 1 * HEADS : 2 * HEADS]
         mean = bn_cols[:, 2 * HEADS : 3 * HEADS]
         variance = bn_cols[:, 3 * HEADS : 4 * HEADS]
-        bn_std = keep.tile([P, HEADS], F32)
-        nc.vector.tensor_scalar_add(out=bn_std[:], in0=variance, scalar1=EPS)
-        nc.scalar.activation(out=bn_std[:], in_=bn_std[:], func=ACT.Sqrt)
+        bn_var = keep.tile([P, HEADS], F32)
+        nc.vector.tensor_scalar_add(out=bn_var[:], in0=variance, scalar1=EPS)
+        minus_half = keep.tile([P, HEADS], F32)
+        nc.gpsimd.memset(minus_half[:], -0.5)
         bn_scale = keep.tile([P, HEADS], F32)
-        nc.vector.reciprocal(out=bn_scale[:], in_=bn_std[:])
-        nc.vector.tensor_mul(out=bn_scale[:], in0=bn_scale[:], in1=gain)
+        nc.gpsimd.tensor_tensor(out=bn_scale[:], in0=bn_var[:], in1=minus_half[:], op=ALU.pow)
         bn_shift = keep.tile([P, HEADS], F32)
-        nc.vector.tensor_mul(out=bn_shift[:], in0=mean, in1=bn_scale[:])
-        nc.vector.tensor_sub(out=bn_shift[:], in0=shift, in1=bn_shift[:])
+
+        def fold_batch_norm():
+            nc.vector.tensor_mul(out=bn_scale[:], in0=bn_scale[:], in1=gain)
+            nc.vector.tensor_mul(out=bn_shift[:], in0=mean, in1=bn_scale[:])
+            nc.vector.tensor_sub(out=bn_shift[:], in0=shift, in1=bn_shift[:])
 
         s_banks = {}
         rows = {WEIGHTS: w_sb}
@@ -161,37 +164,34 @@ def tile_bottleneck_transformer_pa_t_kernel(
         def group_rows(j, half):
             if not has_rows(j):
                 return
-            side_by_side = work.tile([P, 2, P, PACK], BF16, bufs=4, align_bytes=64)
-            grouped[(j, half)] = side_by_side
-            alternately = flipped[(j, half)][:].rearrange("p a u r -> p a r u")
-            as_words = side_by_side[:].rearrange("p a r t -> p (a r t)").bitcast(F32)
-            as_words = as_words.rearrange("p (a r u) -> p a r u", a=2, u=2)
             if half == 0:
-                nc.scalar.copy(out=as_words, in_=alternately)
-            else:
-                nc.vector.tensor_copy(out=as_words, in_=alternately)
+                side_by_side = work.tile([P, TILES, P, PACK], BF16, bufs=3, align_bytes=64)
+                grouped[j] = side_by_side
+            alternately = flipped[(j, half)][:].rearrange("p a u r -> p a r u")
+            as_words = grouped[j][:, 2 * half : 2 * half + 2, :, :].rearrange("p a r t -> p (a r t)").bitcast(F32)
+            as_words = as_words.rearrange("p (a r u) -> p a r u", a=2, u=2)
+            nc.scalar.copy(out=as_words, in_=alternately)
 
-        def quantise_rows(j, half):
+        def quantise_rows(j):
             if not has_rows(j):
                 return
             if j == WEIGHTS:
-                words = keep.tile([P, 2 * P], U32, name="w_words%d" % half, align_bytes=64)
-                plane = keep.tile([P, 2 * P], U8, name="w_plane%d" % half, align_bytes=64)
+                words = keep.tile([P, TILES * P], U32, name="w_words", align_bytes=64)
+                plane = keep.tile([P, TILES * P], U8, name="w_plane", align_bytes=64)
             else:
-                words = work.tile([P, 2 * P], U32, bufs=4, align_bytes=64)
-                plane = work.tile([P, 2 * P], U8, bufs=4, align_bytes=64)
-            codes[(j, half)] = words
-            scales[(j, half)] = plane
+                words = work.tile([P, TILES * P], U32, bufs=3, align_bytes=64)
+                plane = work.tile([P, TILES * P], U8, bufs=3, align_bytes=64)
+            codes[j] = words
+            scales[j] = plane
             nc.vector.quantize_mx(
                 out=words[:].bitcast(FP8X4),
                 scales=plane[:],
-                in_=grouped[(j, half)][:].rearrange("p a r t -> p (a r t)"),
+                in_=grouped[j][:].rearrange("p a r t -> p (a r t)"),
             )
 
         def row_tile_operand(j, nt):
-            half, a = divmod(nt, 2)
-            cols = slice(a * P, (a + 1) * P)
-            return codes[(j, half)][:, cols].bitcast(FP8X4), scales[(j, half)][:, cols]
+            cols = slice(nt * P, (nt + 1) * P)
+            return codes[j][:, cols].bitcast(FP8X4), scales[j][:, cols]
 
         def group_h1(g):
             if not 0 <= g < BATCH * TILES:
@@ -293,10 +293,12 @@ def tile_bottleneck_transformer_pa_t_kernel(
             nc.vector.reciprocal(out=inv_sum[:], in_=row_sum[j][:])
             ot_rows = work.tile([P, TILES, P], F32, bufs=2)
             o_rows[j] = ot_rows
-            for nt in range(TILES):
-                nc.scalar.activation(
-                    out=ot_rows[:, nt, :], in_=o_bank[j][:, nt, :], func=ACT.Copy, scale=inv_sum[:, nt : nt + 1]
-                )
+            nc.vector.tensor_tensor(
+                out=ot_rows[:],
+                in0=o_bank[j][:],
+                in1=inv_sum[:].unsqueeze(2).to_broadcast([P, TILES, P]),
+                op=ALU.mult,
+            )
 
         def flip_back(j):
             if not is_pair(j):
@@ -327,14 +329,13 @@ def tile_bottleneck_transformer_pa_t_kernel(
             group_h1(i + TILES)
 
             scores(i, 1)
-            quantise_rows(i - 2, 0)
             bias_v(i - 2)
             softmax(i, 1)
             group_rows(i - 1, 0)
 
             scores(i, 2)
             flip_back(i - 3)
-            quantise_rows(i - 2, 1)
+            quantise_rows(i - 2)
             quantise_v(i - 2)
             softmax(i, 2)
             finish(i - 3)
@@ -349,3 +350,5 @@ def tile_bottleneck_transformer_pa_t_kernel(
             if i == 0:
                 for g in range(TILES):
                     quantise_h1(g)
+            if i == 2:
+                fold_batch_norm()

@@ -294,10 +294,16 @@ def tile_bottleneck_transformer_pa_t_kernel(
             ot_rows = work.tile([P, TILES, P], F32, bufs=2)
             o_rows[j] = ot_rows
             nc.vector.tensor_tensor(
-                out=ot_rows[:],
-                in0=o_bank[j][:],
-                in1=inv_sum[:].unsqueeze(2).to_broadcast([P, TILES, P]),
+                out=ot_rows[:, 0 : TILES - 1, :],
+                in0=o_bank[j][:, 0 : TILES - 1, :],
+                in1=inv_sum[:, 0 : TILES - 1].unsqueeze(2).to_broadcast([P, TILES - 1, P]),
                 op=ALU.mult,
+            )
+            nc.scalar.activation(
+                out=ot_rows[:, TILES - 1, :],
+                in_=o_bank[j][:, TILES - 1, :],
+                func=ACT.Copy,
+                scale=inv_sum[:, TILES - 1 : TILES],
             )
 
         def flip_back(j):

@@ -79,21 +79,23 @@ def tile_bottleneck_transformer_pa_t_kernel(
         ident_f32 = keep.tile([P, P], F32)
         make_identity(nc, ident_f32[:])
 
-        bn_flipped = psum.tile([P, P], BF16, tag="back", bufs=1)
-        nc.tensor.transpose(out=bn_flipped[:], in_=bn_rows[:], identity=ident_bf[:])
         bn_cols = keep.tile([P, 4 * HEADS], F32)
-        nc.vector.tensor_copy(out=bn_cols[:], in_=bn_flipped[:, 0 : 4 * HEADS])
         gain = bn_cols[:, 0 * HEADS : 1 * HEADS]
         shift = bn_cols[:, 1 * HEADS : 2 * HEADS]
         mean = bn_cols[:, 2 * HEADS : 3 * HEADS]
         variance = bn_cols[:, 3 * HEADS : 4 * HEADS]
         bn_var = keep.tile([P, HEADS], F32)
-        nc.vector.tensor_scalar_add(out=bn_var[:], in0=variance, scalar1=EPS)
         minus_half = keep.tile([P, HEADS], F32)
         nc.gpsimd.memset(minus_half[:], -0.5)
         bn_scale = keep.tile([P, HEADS], F32)
-        nc.gpsimd.tensor_tensor(out=bn_scale[:], in0=bn_var[:], in1=minus_half[:], op=ALU.pow)
         bn_shift = keep.tile([P, HEADS], F32)
+
+        def flip_batch_norm():
+            bn_flipped = psum.tile([P, P], BF16, tag="bank", bufs=8)
+            nc.tensor.transpose(out=bn_flipped[:], in_=bn_rows[:], identity=ident_bf[:])
+            nc.vector.tensor_copy(out=bn_cols[:], in_=bn_flipped[:, 0 : 4 * HEADS])
+            nc.vector.tensor_scalar_add(out=bn_var[:], in0=variance, scalar1=EPS)
+            nc.gpsimd.tensor_tensor(out=bn_scale[:], in0=bn_var[:], in1=minus_half[:], op=ALU.pow)
 
         def fold_batch_norm():
             nc.vector.tensor_mul(out=bn_scale[:], in0=bn_scale[:], in1=gain)
@@ -120,7 +122,7 @@ def tile_bottleneck_transformer_pa_t_kernel(
             if is_pair(i):
                 b, h = divmod(i, HEADS)
                 n_cols = slice(nt * P, (nt + 1) * P)
-                s_bank = psum.tile([P, POSITIONS], F32, tag="scores", bufs=3)
+                s_bank = psum.tile([P, POSITIONS], F32, tag="bank", bufs=8)
                 s_banks[(i, nt)] = s_bank
                 nc.tensor.matmul(
                     out=s_bank[:], lhsT=q_sb[b][:, h, n_cols], rhs=k_sb[b][:, h, :], start=True, stop=False
@@ -153,7 +155,7 @@ def tile_bottleneck_transformer_pa_t_kernel(
         def flip(j, nt):
             half, a = divmod(nt, 2)
             if a == 0:
-                flip_bank = psum.tile([P, 2, 2, P], F32, tag="flipped", bufs=2)
+                flip_bank = psum.tile([P, 2, 2, P], F32, tag="bank", bufs=8)
                 flipped[(j, half)] = flip_bank
             words = rows[j][:, nt, :].bitcast(F32)
             for u in range(2):
@@ -230,7 +232,7 @@ def tile_bottleneck_transformer_pa_t_kernel(
             if not is_pair(j):
                 return
             b, h = divmod(j, HEADS)
-            vt_bank = psum.tile([P, TILES, P], F32, tag="mx", bufs=2)
+            vt_bank = psum.tile([P, TILES, P], F32, tag="bank", bufs=8)
             v_bank[j] = vt_bank
             w_words, w_plane = row_tile_operand(WEIGHTS, h)
             for mt in range(TILES):
@@ -272,7 +274,7 @@ def tile_bottleneck_transformer_pa_t_kernel(
         def attend(j):
             if not is_pair(j):
                 return
-            ot_bank = psum.tile([P, TILES, P], F32, tag="mx", bufs=2)
+            ot_bank = psum.tile([P, TILES, P], F32, tag="bank", bufs=8)
             o_bank[j] = ot_bank
             for nt in range(TILES):
                 e_words, e_plane = row_tile_operand(j, nt)
@@ -309,7 +311,7 @@ def tile_bottleneck_transformer_pa_t_kernel(
         def flip_back(j):
             if not is_pair(j):
                 return
-            back_bank = psum.tile([P, POSITIONS], F32, tag="back", bufs=1)
+            back_bank = psum.tile([P, POSITIONS], F32, tag="bank", bufs=8)
             o_back[j] = back_bank
             for nt in range(TILES):
                 nc.tensor.transpose(
@@ -356,5 +358,6 @@ def tile_bottleneck_transformer_pa_t_kernel(
             if i == 0:
                 for g in range(TILES):
                     quantise_h1(g)
+                flip_batch_norm()
             if i == 2:
                 fold_batch_norm()

@@ -59,6 +59,7 @@ def tile_bottleneck_transformer_pa_t_kernel(
                 )
 
         load_first_batch_head(0)
+        load_h1(0)
         nc.sync.dma_start(out=w_sb[:], in_=v_w.rearrange("(c p) i -> p c i", p=P))
         nc.vector.memset(bn_rows[:], 0.0)
         for r, vec in enumerate((bn2_g, bn2_b, bn2_m, bn2_v)):
@@ -68,7 +69,6 @@ def tile_bottleneck_transformer_pa_t_kernel(
         nc.scalar.dma_start(out=vb_all[:], in_=v_b.partition_broadcast(P))
         for h in range(1, HEADS):
             load_first_batch_head(h)
-        load_h1(0)
         for b in range(1, BATCH):
             nc.sync.dma_start(out=q_sb[b][:], in_=q[b].rearrange("(h d) n -> d h n", h=HEADS))
             nc.sync.dma_start(out=k_sb[b][:], in_=k[b].rearrange("(h d) n -> d h n", h=HEADS))
@@ -104,12 +104,12 @@ def tile_bottleneck_transformer_pa_t_kernel(
 
         s_banks = {}
         rows = {WEIGHTS: w_sb}
-        row_sum = {}
+        row_sums, inverse = {}, {}
         flipped = {}
         grouped = {}
         codes, scales = {}, {}
         h_grouped, h_codes, h_scales = {}, {}, {}
-        v_bank, v_grouped, v_codes, v_scales = {}, {}, {}, {}
+        v_bank, vh_grouped, v_codes, v_scales = {}, {}, {}, {}
         o_bank, o_rows, o_back = {}, {}, {}
 
         def is_pair(j):
@@ -117,6 +117,12 @@ def tile_bottleneck_transformer_pa_t_kernel(
 
         def has_rows(j):
             return j == WEIGHTS or is_pair(j)
+
+        def copy_units(j):
+            return [(0, 2), (2, 1), (3, 1)] if j == PAIRS - 1 else [(0, 2), (2, 2)]
+
+        def late_units(j):
+            return copy_units(j) if j == PAIRS - 1 else [(0, TILES)]
 
         def scores(i, nt):
             if is_pair(i):
@@ -130,7 +136,7 @@ def tile_bottleneck_transformer_pa_t_kernel(
                 nc.tensor.matmul(
                     out=s_bank[:], lhsT=pos_sb[:, h, n_cols], rhs=q_sb[b][:, h, :], start=False, stop=True
                 )
-            if has_rows(i - 1):
+            if is_pair(i - 1):
                 flip(i - 1, nt)
 
         def softmax(i, nt):
@@ -139,8 +145,9 @@ def tile_bottleneck_transformer_pa_t_kernel(
             if nt == 0:
                 e_rows = work.tile([P, TILES, POSITIONS], BF16, bufs=3)
                 rows[i] = e_rows
-                e_sum = work.tile([P, TILES], F32, bufs=4)
-                row_sum[i] = e_sum
+                if i % 2 == 0:
+                    e_sums = work.tile([P, 2 * TILES], F32, bufs=3)
+                    row_sums[i // 2] = e_sums
             neg_max = work.tile([P, 1], F32, bufs=4)
             nc.vector.tensor_reduce(out=neg_max[:], in_=s_banks[(i, nt)][:], axis=AXIS.X, op=ALU.max, negate=True)
             nc.scalar.activation(
@@ -149,18 +156,18 @@ def tile_bottleneck_transformer_pa_t_kernel(
                 func=ACT.Exp,
                 bias=neg_max[:],
                 scale=1.0,
-                accum_out=row_sum[i][:, nt : nt + 1],
+                accum_out=row_sums[i // 2][:, (i % 2) * TILES + nt : (i % 2) * TILES + nt + 1],
             )
 
         def flip(j, nt):
-            half, a = divmod(nt, 2)
-            if a == 0:
-                flip_bank = psum.tile([P, 2, 2, P], F32, tag="bank", bufs=8)
-                flipped[(j, half)] = flip_bank
+            first, count = [unit for unit in copy_units(j) if unit[0] <= nt < unit[0] + unit[1]][0]
+            if nt == first:
+                flip_bank = psum.tile([P, count, 2, P], F32, tag="bank", bufs=8)
+                flipped[(j, first)] = flip_bank
             words = rows[j][:, nt, :].bitcast(F32)
             for u in range(2):
                 nc.tensor.transpose(
-                    out=flipped[(j, half)][:, a, u, :], in_=words[:, u * P : (u + 1) * P], identity=ident_f32[:]
+                    out=flipped[(j, first)][:, nt - first, u, :], in_=words[:, u * P : (u + 1) * P], identity=ident_f32[:]
                 )
 
         def group_rows(j, half):
@@ -169,10 +176,12 @@ def tile_bottleneck_transformer_pa_t_kernel(
             if half == 0:
                 side_by_side = work.tile([P, TILES, P, PACK], BF16, bufs=3, align_bytes=64)
                 grouped[j] = side_by_side
-            alternately = flipped[(j, half)][:].rearrange("p a u r -> p a r u")
-            as_words = grouped[j][:, 2 * half : 2 * half + 2, :, :].rearrange("p a r t -> p (a r t)").bitcast(F32)
-            as_words = as_words.rearrange("p (a r u) -> p a r u", a=2, u=2)
-            nc.scalar.copy(out=as_words, in_=alternately)
+            for first, count in copy_units(j):
+                if first // 2 == half:
+                    alternately = flipped[(j, first)][:].rearrange("p a u r -> p a r u")
+                    as_words = grouped[j][:, first : first + count, :, :].rearrange("p a r t -> p (a r t)").bitcast(F32)
+                    as_words = as_words.rearrange("p (a r u) -> p a r u", a=count, u=2)
+                    nc.scalar.copy(out=as_words, in_=alternately)
 
         def quantise_rows(j):
             if not has_rows(j):
@@ -185,24 +194,36 @@ def tile_bottleneck_transformer_pa_t_kernel(
                 plane = work.tile([P, TILES * P], U8, bufs=3, align_bytes=64)
             codes[j] = words
             scales[j] = plane
-            nc.vector.quantize_mx(
-                out=words[:].bitcast(FP8X4),
-                scales=plane[:],
-                in_=grouped[j][:].rearrange("p a r t -> p (a r t)"),
-            )
+            for first, count in late_units(j):
+                cols = slice(first * P, (first + count) * P)
+                nc.vector.quantize_mx(
+                    out=words[:, cols].bitcast(FP8X4),
+                    scales=plane[:, cols],
+                    in_=grouped[j][:, first : first + count, :, :].rearrange("p a r t -> p (a r t)"),
+                )
 
         def row_tile_operand(j, nt):
             cols = slice(nt * P, (nt + 1) * P)
             return codes[j][:, cols].bitcast(FP8X4), scales[j][:, cols]
 
+        def v_and_h1(r):
+            if r not in vh_grouped:
+                vh_side = work.tile([P, 2, P, PACK], BF16, bufs=6, align_bytes=64)
+                vh_grouped[r] = vh_side
+            return vh_grouped[r]
+
         def group_h1(g):
             if not 0 <= g < BATCH * TILES:
                 return
             b, mt = divmod(g, TILES)
-            h_side = work.tile([P, P, PACK], BF16, bufs=6, align_bytes=64)
-            h_grouped[g] = h_side
+            if b == 0:
+                h_first = work.tile([P, P, PACK], BF16, bufs=4, align_bytes=64)
+                h_side = h_first[:]
+                h_grouped[g] = h_first
+            else:
+                h_side = v_and_h1(g - TILES + 1)[:, 1, :, :]
             nc.gpsimd.tensor_scalar(
-                out=h_side[:].rearrange("p (c i) t -> p c t i", i=4),
+                out=h_side.rearrange("p (c i) t -> p c t i", i=4),
                 in0=h_sb[b][:, :, 2 * P * (mt // 2) + mt % 2 : 2 * P * (mt // 2 + 1) : 2].rearrange(
                     "p t (c i) -> p c t i", i=4
                 ),
@@ -212,20 +233,29 @@ def tile_bottleneck_transformer_pa_t_kernel(
                 op1=ALU.add,
             )
 
-        def quantise_h1(g):
-            if not 0 <= g < BATCH * TILES:
-                return
-            b, mt = divmod(g, TILES)
-            if mt == 0:
-                h_words = work.tile([P, POSITIONS], U32, bufs=3, align_bytes=64)
-                h_plane = work.tile([P, POSITIONS], U8, bufs=3, align_bytes=64)
-                h_codes[b] = h_words
-                h_scales[b] = h_plane
-            m_cols = slice(mt * P, (mt + 1) * P)
+        def quantise_first_h1(g):
+            h_words = keep.tile([P, P], U32, name="h_words%d" % g, align_bytes=64)
+            h_plane = keep.tile([P, P], U8, name="h_plane%d" % g, align_bytes=64)
+            h_codes[g] = h_words[:]
+            h_scales[g] = h_plane[:]
             nc.vector.quantize_mx(
-                out=h_codes[b][:, m_cols].bitcast(FP8X4),
-                scales=h_scales[b][:, m_cols],
-                in_=h_grouped[g][:].rearrange("p m t -> p (m t)"),
+                out=h_words[:].bitcast(FP8X4), scales=h_plane[:], in_=h_grouped[g][:].rearrange("p m t -> p (m t)")
+            )
+
+        def quantise_v_and_h1(r):
+            j, g = r - 2, r + TILES - 1
+            parts = [part for part, there in ((0, is_pair(j)), (1, TILES <= g < BATCH * TILES)) if there]
+            if not parts:
+                return
+            vh_words = work.tile([P, 2 * P], U32, bufs=10, align_bytes=64)
+            vh_plane = work.tile([P, 2 * P], U8, bufs=10, align_bytes=64)
+            v_codes[j], v_scales[j] = vh_words[:, 0:P], vh_plane[:, 0:P]
+            h_codes[g], h_scales[g] = vh_words[:, P : 2 * P], vh_plane[:, P : 2 * P]
+            cols = slice(parts[0] * P, (parts[-1] + 1) * P)
+            nc.vector.quantize_mx(
+                out=vh_words[:, cols].bitcast(FP8X4),
+                scales=vh_plane[:, cols],
+                in_=vh_grouped[r][:, parts[0] : parts[-1] + 1, :, :].rearrange("p s m t -> p (s m t)"),
             )
 
         def project_v(j):
@@ -236,11 +266,10 @@ def tile_bottleneck_transformer_pa_t_kernel(
             v_bank[j] = vt_bank
             w_words, w_plane = row_tile_operand(WEIGHTS, h)
             for mt in range(TILES):
-                m_cols = slice(mt * P, (mt + 1) * P)
                 nc.tensor.matmul_mx(
                     out=vt_bank[:, mt, :],
-                    lhsT=h_codes[b][:, m_cols].bitcast(FP8X4),
-                    lhsT_scale=h_scales[b][:, m_cols],
+                    lhsT=h_codes[TILES * b + mt].bitcast(FP8X4),
+                    lhsT_scale=h_scales[TILES * b + mt],
                     rhs=w_words,
                     rhs_scale=w_plane,
                     start=True,
@@ -251,82 +280,85 @@ def tile_bottleneck_transformer_pa_t_kernel(
             if not is_pair(j):
                 return
             h = j % HEADS
-            v_side = work.tile([P, P, PACK], BF16, bufs=2, align_bytes=64)
-            v_grouped[j] = v_side
             nc.vector.tensor_tensor(
-                out=v_side[:],
+                out=v_and_h1(j + 2)[:, 0, :, :],
                 in0=v_bank[j][:].rearrange("p t d -> p d t"),
                 in1=vb_all[:, h * P : (h + 1) * P].unsqueeze(2).to_broadcast([P, P, PACK]),
                 op=ALU.add,
             )
 
-        def quantise_v(j):
-            if not is_pair(j):
-                return
-            v_words = work.tile([P, P], U32, bufs=3, align_bytes=64)
-            v_plane = work.tile([P, P], U8, bufs=3, align_bytes=64)
-            v_codes[j] = v_words
-            v_scales[j] = v_plane
-            nc.vector.quantize_mx(
-                out=v_words[:].bitcast(FP8X4), scales=v_plane[:], in_=v_grouped[j][:].rearrange("p d t -> p (d t)")
-            )
-
         def attend(j):
             if not is_pair(j):
                 return
-            ot_bank = psum.tile([P, TILES, P], F32, tag="bank", bufs=8)
-            o_bank[j] = ot_bank
-            for nt in range(TILES):
-                e_words, e_plane = row_tile_operand(j, nt)
-                nc.tensor.matmul_mx(
-                    out=ot_bank[:, nt, :],
-                    lhsT=e_words,
-                    lhsT_scale=e_plane,
-                    rhs=v_codes[j][:].bitcast(FP8X4),
-                    rhs_scale=v_scales[j][:],
-                    start=True,
-                    stop=True,
-                )
+            for first, count in late_units(j):
+                ot_bank = psum.tile([P, count, P], F32, tag="bank", bufs=8)
+                o_bank[(j, first)] = ot_bank
+                for a in range(count):
+                    e_words, e_plane = row_tile_operand(j, first + a)
+                    nc.tensor.matmul_mx(
+                        out=ot_bank[:, a, :],
+                        lhsT=e_words,
+                        lhsT_scale=e_plane,
+                        rhs=v_codes[j].bitcast(FP8X4),
+                        rhs_scale=v_scales[j],
+                        start=True,
+                        stop=True,
+                    )
+
+        def invert_sums(j):
+            if not is_pair(j) or j % 2 == 1:
+                return
+            inv_sums = work.tile([P, 2 * TILES], F32, bufs=3)
+            inverse[j // 2] = inv_sums
+            nc.vector.reciprocal(out=inv_sums[:], in_=row_sums[j // 2][:])
 
         def normalise(j):
             if not is_pair(j):
                 return
-            inv_sum = work.tile([P, TILES], F32, bufs=2)
-            nc.vector.reciprocal(out=inv_sum[:], in_=row_sum[j][:])
+            inv_sum = inverse[j // 2][:, (j % 2) * TILES : (j % 2 + 1) * TILES]
             ot_rows = work.tile([P, TILES, P], F32, bufs=2)
             o_rows[j] = ot_rows
-            nc.vector.tensor_tensor(
-                out=ot_rows[:, 0 : TILES - 1, :],
-                in0=o_bank[j][:, 0 : TILES - 1, :],
-                in1=inv_sum[:, 0 : TILES - 1].unsqueeze(2).to_broadcast([P, TILES - 1, P]),
-                op=ALU.mult,
-            )
-            nc.scalar.activation(
-                out=ot_rows[:, TILES - 1, :],
-                in_=o_bank[j][:, TILES - 1, :],
-                func=ACT.Copy,
-                scale=inv_sum[:, TILES - 1 : TILES],
-            )
+            for first, count in late_units(j):
+                by_vector = count - 1 if count == TILES and j % 2 == 1 else count
+                nc.vector.tensor_tensor(
+                    out=ot_rows[:, first : first + by_vector, :],
+                    in0=o_bank[(j, first)][:, 0:by_vector, :],
+                    in1=inv_sum[:, first : first + by_vector].unsqueeze(2).to_broadcast([P, by_vector, P]),
+                    op=ALU.mult,
+                )
+                for a in range(by_vector, count):
+                    nc.scalar.activation(
+                        out=ot_rows[:, first + a, :],
+                        in_=o_bank[(j, first)][:, a, :],
+                        func=ACT.Copy,
+                        scale=inv_sum[:, first + a : first + a + 1],
+                    )
 
         def flip_back(j):
             if not is_pair(j):
                 return
-            back_bank = psum.tile([P, POSITIONS], F32, tag="bank", bufs=8)
-            o_back[j] = back_bank
-            for nt in range(TILES):
-                nc.tensor.transpose(
-                    out=back_bank[:, nt * P : (nt + 1) * P], in_=o_rows[j][:, nt, :], identity=ident_f32[:]
-                )
+            for first, count in late_units(j):
+                back_bank = psum.tile([P, count * P], F32, tag="bank", bufs=8)
+                o_back[(j, first)] = back_bank
+                for a in range(count):
+                    nc.tensor.transpose(
+                        out=back_bank[:, a * P : (a + 1) * P], in_=o_rows[j][:, first + a, :], identity=ident_f32[:]
+                    )
 
         def finish(j):
             if not is_pair(j):
                 return
             b, h = divmod(j, HEADS)
-            y = work.tile([P, POSITIONS], F32, bufs=4)
-            nc.scalar.activation(
-                out=y[:], in_=o_back[j][:], func=ACT.Relu, bias=bn_shift[:, h : h + 1], scale=bn_scale[:, h : h + 1]
-            )
-            nc.sync.dma_start(out=out[b, h * P : (h + 1) * P, :], in_=y[:])
+            for first, count in late_units(j):
+                y = work.tile([P, count * P], F32, bufs=4)
+                nc.scalar.activation(
+                    out=y[:],
+                    in_=o_back[(j, first)][:],
+                    func=ACT.Relu,
+                    bias=bn_shift[:, h : h + 1],
+                    scale=bn_scale[:, h : h + 1],
+                )
+                nc.sync.dma_start(out=out[b, h * P : (h + 1) * P, first * P : (first + count) * P], in_=y[:])
 
         for g in range(TILES):
             group_h1(g)
@@ -338,26 +370,31 @@ def tile_bottleneck_transformer_pa_t_kernel(
 
             scores(i, 1)
             bias_v(i - 2)
+            invert_sums(i - 2)
             softmax(i, 1)
-            group_rows(i - 1, 0)
+            if i > 0:
+                group_rows(i - 1, 0)
 
             scores(i, 2)
             flip_back(i - 3)
             quantise_rows(i - 2)
-            quantise_v(i - 2)
+            quantise_v_and_h1(i)
             softmax(i, 2)
             finish(i - 3)
 
             scores(i, 3)
+            if i == 0:
+                for nt in range(TILES):
+                    flip(WEIGHTS, nt)
+                group_rows(WEIGHTS, 0)
+            if i == 1:
+                for g in range(TILES):
+                    quantise_first_h1(g)
             attend(i - 2)
             project_v(i - 1)
-            if i > 0:
-                quantise_h1(i + TILES - 1)
             softmax(i, 3)
             normalise(i - 2)
             if i == 0:
-                for g in range(TILES):
-                    quantise_h1(g)
                 flip_batch_norm()
             if i == 2:
                 fold_batch_norm()

@@ -49,7 +49,8 @@ def tile_bottleneck_transformer_pa_t_kernel(
             d_rows = slice(h * P, (h + 1) * P)
             nc.sync.dma_start(out=q_sb[0][:, h, :], in_=q[0, d_rows, :])
             nc.sync.dma_start(out=k_sb[0][:, h, :], in_=k[0, d_rows, :])
-            nc.sync.dma_start(out=pos_sb[:, h, :], in_=pos[h])
+            pos_queue = nc.scalar if h == 0 else nc.sync
+            pos_queue.dma_start(out=pos_sb[:, h, :], in_=pos[h])
 
         def load_h1(b):
             for u in range(2):
@@ -61,7 +62,7 @@ def tile_bottleneck_transformer_pa_t_kernel(
         load_first_batch_head(0)
         load_h1(0)
         nc.sync.dma_start(out=w_sb[:], in_=v_w.rearrange("(c p) i -> p c i", p=P))
-        nc.vector.memset(bn_rows[:], 0.0)
+        nc.gpsimd.memset(bn_rows[:], 0.0)
         for r, vec in enumerate((bn2_g, bn2_b, bn2_m, bn2_v)):
             nc.scalar.dma_start(
                 out=bn_rows[r * HEADS : (r + 1) * HEADS, :], in_=vec.rearrange("(h d) -> h d", h=HEADS)
@@ -94,13 +95,13 @@ def tile_bottleneck_transformer_pa_t_kernel(
             bn_flipped = psum.tile([P, P], BF16, tag="bank", bufs=8)
             nc.tensor.transpose(out=bn_flipped[:], in_=bn_rows[:], identity=ident_bf[:])
             nc.vector.tensor_copy(out=bn_cols[:], in_=bn_flipped[:, 0 : 4 * HEADS])
-            nc.vector.tensor_scalar_add(out=bn_var[:], in0=variance, scalar1=EPS)
+            nc.gpsimd.tensor_scalar_add(out=bn_var[:], in0=variance, scalar1=EPS)
             nc.gpsimd.tensor_tensor(out=bn_scale[:], in0=bn_var[:], in1=minus_half[:], op=ALU.pow)
 
         def fold_batch_norm():
-            nc.vector.tensor_mul(out=bn_scale[:], in0=bn_scale[:], in1=gain)
-            nc.vector.tensor_mul(out=bn_shift[:], in0=mean, in1=bn_scale[:])
-            nc.vector.tensor_sub(out=bn_shift[:], in0=shift, in1=bn_shift[:])
+            nc.gpsimd.tensor_mul(out=bn_scale[:], in0=bn_scale[:], in1=gain)
+            nc.gpsimd.tensor_mul(out=bn_shift[:], in0=mean, in1=bn_scale[:])
+            nc.gpsimd.tensor_sub(out=bn_shift[:], in0=shift, in1=bn_shift[:])
 
         s_banks = {}
         rows = {WEIGHTS: w_sb}
@@ -108,7 +109,7 @@ def tile_bottleneck_transformer_pa_t_kernel(
         flipped = {}
         grouped = {}
         codes, scales = {}, {}
-        h_grouped, h_codes, h_scales = {}, {}, {}
+        h_codes, h_scales = {}, {}
         v_bank, vh_grouped, v_codes, v_scales = {}, {}, {}, {}
         o_bank, o_rows, o_back = {}, {}, {}
 
@@ -206,6 +207,8 @@ def tile_bottleneck_transformer_pa_t_kernel(
             cols = slice(nt * P, (nt + 1) * P)
             return codes[j][:, cols].bitcast(FP8X4), scales[j][:, cols]
 
+        h_first = keep.tile([P, TILES, P, PACK], BF16, align_bytes=64)
+
         def v_and_h1(r):
             if r not in vh_grouped:
                 vh_side = work.tile([P, 2, P, PACK], BF16, bufs=6, align_bytes=64)
@@ -217,9 +220,7 @@ def tile_bottleneck_transformer_pa_t_kernel(
                 return
             b, mt = divmod(g, TILES)
             if b == 0:
-                h_first = work.tile([P, P, PACK], BF16, bufs=4, align_bytes=64)
-                h_side = h_first[:]
-                h_grouped[g] = h_first
+                h_side = h_first[:, mt, :, :]
             else:
                 h_side = v_and_h1(g - TILES + 1)[:, 1, :, :]
             nc.gpsimd.tensor_scalar(
@@ -233,13 +234,14 @@ def tile_bottleneck_transformer_pa_t_kernel(
                 op1=ALU.add,
             )
 
-        def quantise_first_h1(g):
-            h_words = keep.tile([P, P], U32, name="h_words%d" % g, align_bytes=64)
-            h_plane = keep.tile([P, P], U8, name="h_plane%d" % g, align_bytes=64)
-            h_codes[g] = h_words[:]
-            h_scales[g] = h_plane[:]
+        def quantise_first_h1():
+            h_words = keep.tile([P, TILES * P], U32, align_bytes=64)
+            h_plane = keep.tile([P, TILES * P], U8, align_bytes=64)
+            for g in range(TILES):
+                h_codes[g] = h_words[:, g * P : (g + 1) * P]
+                h_scales[g] = h_plane[:, g * P : (g + 1) * P]
             nc.vector.quantize_mx(
-                out=h_words[:].bitcast(FP8X4), scales=h_plane[:], in_=h_grouped[g][:].rearrange("p m t -> p (m t)")
+                out=h_words[:].bitcast(FP8X4), scales=h_plane[:], in_=h_first[:].rearrange("p g m t -> p (g m t)")
             )
 
         def quantise_v_and_h1(r):
@@ -388,8 +390,7 @@ def tile_bottleneck_transformer_pa_t_kernel(
                     flip(WEIGHTS, nt)
                 group_rows(WEIGHTS, 0)
             if i == 1:
-                for g in range(TILES):
-                    quantise_first_h1(g)
+                quantise_first_h1()
             attend(i - 2)
             project_v(i - 1)
             softmax(i, 3)

from contextlib import ExitStack

import concourse.mybir as mybir
from concourse.masks import make_identity

BF16 = mybir.dt.bfloat16
F32 = mybir.dt.float32
U32 = mybir.dt.uint32
U8 = mybir.dt.uint8
FP8X4 = mybir.dt.float8_e4m3fn_x4
ACT = mybir.ActivationFunctionType
ALU = mybir.AluOpType
AXIS = mybir.AxisListType

P = 128
PACK = 4
BATCH = 8
HEADS = 4
CHANNELS = HEADS * P
POSITIONS = PACK * P
TILES = POSITIONS // P
PAIRS = BATCH * HEADS
WEIGHTS = -1
EPS = 1e-5

FLOPS = 2 * (BATCH * CHANNELS * CHANNELS * POSITIONS + 3 * PAIRS * P * POSITIONS * POSITIONS)


def tile_bottleneck_transformer_pa_t_kernel(
    tc, h1, v_w, v_b, q, k, pos, bn2_g, bn2_b, bn2_m, bn2_v, out
):
    nc = tc.nc
    with ExitStack() as ctx:
        keep = ctx.enter_context(tc.tile_pool(name="keep", bufs=1))
        work = ctx.enter_context(tc.tile_pool(name="work", bufs=2))
        psum = ctx.enter_context(tc.psum_pool(name="psum", bufs=1))

        q_sb, k_sb, h_sb = [], [], []
        for b in range(BATCH):
            q_sb.append(keep.tile([P, HEADS, POSITIONS], BF16, name="q%d" % b))
            k_sb.append(keep.tile([P, HEADS, POSITIONS], BF16, name="k%d" % b))
            h_sb.append(keep.tile([P, PACK, POSITIONS], BF16, name="h%d" % b))
        pos_sb = keep.tile([P, HEADS, POSITIONS], BF16)
        w_sb = keep.tile([P, TILES, CHANNELS], BF16)
        bn_rows = keep.tile([P, P], BF16)
        vb_all = keep.tile([P, CHANNELS], BF16)

        def load_first_batch_head(h):
            d_rows = slice(h * P, (h + 1) * P)
            nc.sync.dma_start(out=q_sb[0][:, h, :], in_=q[0, d_rows, :])
            nc.sync.dma_start(out=k_sb[0][:, h, :], in_=k[0, d_rows, :])
            pos_queue = nc.scalar if h == 0 else nc.sync
            pos_queue.dma_start(out=pos_sb[:, h, :], in_=pos[h])

        def load_h1(b):
            for u in range(2):
                nc.sync.dma_start(
                    out=h_sb[b][:, 2 * u : 2 * u + 2, :],
                    in_=h1[b, 2 * P * u : 2 * P * (u + 1), :].rearrange("(p e) m -> p e m", e=2),
                )

        load_first_batch_head(0)
        load_h1(0)
        nc.sync.dma_start(out=w_sb[:], in_=v_w.rearrange("(c p) i -> p c i", p=P))
        nc.gpsimd.memset(bn_rows[:], 0.0)
        for r, vec in enumerate((bn2_g, bn2_b, bn2_m, bn2_v)):
            nc.scalar.dma_start(
                out=bn_rows[r * HEADS : (r + 1) * HEADS, :], in_=vec.rearrange("(h d) -> h d", h=HEADS)
            )
        nc.scalar.dma_start(out=vb_all[:], in_=v_b.partition_broadcast(P))
        for h in range(1, HEADS):
            load_first_batch_head(h)
        for b in range(1, BATCH):
            nc.sync.dma_start(out=q_sb[b][:], in_=q[b].rearrange("(h d) n -> d h n", h=HEADS))
            nc.sync.dma_start(out=k_sb[b][:], in_=k[b].rearrange("(h d) n -> d h n", h=HEADS))
            load_h1(b)

        ident_bf = keep.tile([P, P], BF16)
        make_identity(nc, ident_bf[:])
        ident_f32 = keep.tile([P, P], F32)
        make_identity(nc, ident_f32[:])

        bn_cols = keep.tile([P, 4 * HEADS], F32)
        gain = bn_cols[:, 0 * HEADS : 1 * HEADS]
        shift = bn_cols[:, 1 * HEADS : 2 * HEADS]
        mean = bn_cols[:, 2 * HEADS : 3 * HEADS]
        variance = bn_cols[:, 3 * HEADS : 4 * HEADS]
        bn_var = keep.tile([P, HEADS], F32)
        minus_half = keep.tile([P, HEADS], F32)
        nc.gpsimd.memset(minus_half[:], -0.5)
        bn_scale = keep.tile([P, HEADS], F32)
        bn_shift = keep.tile([P, HEADS], F32)

        def flip_batch_norm():
            bn_flipped = psum.tile([P, P], BF16, tag="bank", bufs=8)
            nc.tensor.transpose(out=bn_flipped[:], in_=bn_rows[:], identity=ident_bf[:])
            nc.vector.tensor_copy(out=bn_cols[:], in_=bn_flipped[:, 0 : 4 * HEADS])
            nc.gpsimd.tensor_scalar_add(out=bn_var[:], in0=variance, scalar1=EPS)
            nc.gpsimd.tensor_tensor(out=bn_scale[:], in0=bn_var[:], in1=minus_half[:], op=ALU.pow)

        def fold_batch_norm():
            nc.gpsimd.tensor_mul(out=bn_scale[:], in0=bn_scale[:], in1=gain)
            nc.gpsimd.tensor_mul(out=bn_shift[:], in0=mean, in1=bn_scale[:])
            nc.gpsimd.tensor_sub(out=bn_shift[:], in0=shift, in1=bn_shift[:])

        s_banks = {}
        rows = {WEIGHTS: w_sb}
        row_sums, inverse = {}, {}
        flipped = {}
        grouped = {}
        codes, scales = {}, {}
        h_codes, h_scales = {}, {}
        v_bank, vh_grouped, v_codes, v_scales = {}, {}, {}, {}
        o_bank, o_rows, o_back = {}, {}, {}

        def is_pair(j):
            return 0 <= j < PAIRS

        def has_rows(j):
            return j == WEIGHTS or is_pair(j)

        def copy_units(j):
            return [(0, 2), (2, 1), (3, 1)] if j == PAIRS - 1 else [(0, 2), (2, 2)]

        def late_units(j):
            return copy_units(j) if j == PAIRS - 1 else [(0, TILES)]

        def scores(i, nt):
            if is_pair(i):
                b, h = divmod(i, HEADS)
                n_cols = slice(nt * P, (nt + 1) * P)
                s_bank = psum.tile([P, POSITIONS], F32, tag="bank", bufs=8)
                s_banks[(i, nt)] = s_bank
                nc.tensor.matmul(
                    out=s_bank[:], lhsT=q_sb[b][:, h, n_cols], rhs=k_sb[b][:, h, :], start=True, stop=False
                )
                nc.tensor.matmul(
                    out=s_bank[:], lhsT=pos_sb[:, h, n_cols], rhs=q_sb[b][:, h, :], start=False, stop=True
                )
            if is_pair(i - 1):
                flip(i - 1, nt)

        def softmax(i, nt):
            if not is_pair(i):
                return
            if nt == 0:
                e_rows = work.tile([P, TILES, POSITIONS], BF16, bufs=3)
                rows[i] = e_rows
                if i % 2 == 0:
                    e_sums = work.tile([P, 2 * TILES], F32, bufs=3)
                    row_sums[i // 2] = e_sums
            neg_max = work.tile([P, 1], F32, bufs=4)
            nc.vector.tensor_reduce(out=neg_max[:], in_=s_banks[(i, nt)][:], axis=AXIS.X, op=ALU.max, negate=True)
            nc.scalar.activation(
                out=rows[i][:, nt, :],
                in_=s_banks[(i, nt)][:],
                func=ACT.Exp,
                bias=neg_max[:],
                scale=1.0,
                accum_out=row_sums[i // 2][:, (i % 2) * TILES + nt : (i % 2) * TILES + nt + 1],
            )

        def flip(j, nt):
            first, count = [unit for unit in copy_units(j) if unit[0] <= nt < unit[0] + unit[1]][0]
            if nt == first:
                flip_bank = psum.tile([P, count, 2, P], F32, tag="bank", bufs=8)
                flipped[(j, first)] = flip_bank
            words = rows[j][:, nt, :].bitcast(F32)
            for u in range(2):
                nc.tensor.transpose(
                    out=flipped[(j, first)][:, nt - first, u, :], in_=words[:, u * P : (u + 1) * P], identity=ident_f32[:]
                )

        def group_rows(j, half):
            if not has_rows(j):
                return
            if half == 0:
                side_by_side = work.tile([P, TILES, P, PACK], BF16, bufs=3, align_bytes=64)
                grouped[j] = side_by_side
            for first, count in copy_units(j):
                if first // 2 == half:
                    alternately = flipped[(j, first)][:].rearrange("p a u r -> p a r u")
                    as_words = grouped[j][:, first : first + count, :, :].rearrange("p a r t -> p (a r t)").bitcast(F32)
                    as_words = as_words.rearrange("p (a r u) -> p a r u", a=count, u=2)
                    nc.scalar.copy(out=as_words, in_=alternately)

        def quantise_rows(j):
            if not has_rows(j):
                return
            if j == WEIGHTS:
                words = keep.tile([P, TILES * P], U32, name="w_words", align_bytes=64)
                plane = keep.tile([P, TILES * P], U8, name="w_plane", align_bytes=64)
            else:
                words = work.tile([P, TILES * P], U32, bufs=3, align_bytes=64)
                plane = work.tile([P, TILES * P], U8, bufs=3, align_bytes=64)
            codes[j] = words
            scales[j] = plane
            for first, count in late_units(j):
                cols = slice(first * P, (first + count) * P)
                nc.vector.quantize_mx(
                    out=words[:, cols].bitcast(FP8X4),
                    scales=plane[:, cols],
                    in_=grouped[j][:, first : first + count, :, :].rearrange("p a r t -> p (a r t)"),
                )

        def row_tile_operand(j, nt):
            cols = slice(nt * P, (nt + 1) * P)
            return codes[j][:, cols].bitcast(FP8X4), scales[j][:, cols]

        h_first = keep.tile([P, TILES, P, PACK], BF16, align_bytes=64)

        def v_and_h1(r):
            if r not in vh_grouped:
                vh_side = work.tile([P, 2, P, PACK], BF16, bufs=6, align_bytes=64)
                vh_grouped[r] = vh_side
            return vh_grouped[r]

        def group_h1(g):
            if not 0 <= g < BATCH * TILES:
                return
            b, mt = divmod(g, TILES)
            if b == 0:
                h_side = h_first[:, mt, :, :]
            else:
                h_side = v_and_h1(g - TILES + 1)[:, 1, :, :]
            nc.gpsimd.tensor_scalar(
                out=h_side.rearrange("p (c i) t -> p c t i", i=4),
                in0=h_sb[b][:, :, 2 * P * (mt // 2) + mt % 2 : 2 * P * (mt // 2 + 1) : 2].rearrange(
                    "p t (c i) -> p c t i", i=4
                ),
                scalar1=1.0,
                scalar2=0.0,
                op0=ALU.mult,
                op1=ALU.add,
            )

        def quantise_first_h1():
            h_words = keep.tile([P, TILES * P], U32, align_bytes=64)
            h_plane = keep.tile([P, TILES * P], U8, align_bytes=64)
            for g in range(TILES):
                h_codes[g] = h_words[:, g * P : (g + 1) * P]
                h_scales[g] = h_plane[:, g * P : (g + 1) * P]
            nc.vector.quantize_mx(
                out=h_words[:].bitcast(FP8X4), scales=h_plane[:], in_=h_first[:].rearrange("p g m t -> p (g m t)")
            )

        def quantise_v_and_h1(r):
            j, g = r - 2, r + TILES - 1
            parts = [part for part, there in ((0, is_pair(j)), (1, TILES <= g < BATCH * TILES)) if there]
            if not parts:
                return
            vh_words = work.tile([P, 2 * P], U32, bufs=10, align_bytes=64)
            vh_plane = work.tile([P, 2 * P], U8, bufs=10, align_bytes=64)
            v_codes[j], v_scales[j] = vh_words[:, 0:P], vh_plane[:, 0:P]
            h_codes[g], h_scales[g] = vh_words[:, P : 2 * P], vh_plane[:, P : 2 * P]
            cols = slice(parts[0] * P, (parts[-1] + 1) * P)
            nc.vector.quantize_mx(
                out=vh_words[:, cols].bitcast(FP8X4),
                scales=vh_plane[:, cols],
                in_=vh_grouped[r][:, parts[0] : parts[-1] + 1, :, :].rearrange("p s m t -> p (s m t)"),
            )

        def project_v(j):
            if not is_pair(j):
                return
            b, h = divmod(j, HEADS)
            vt_bank = psum.tile([P, TILES, P], F32, tag="bank", bufs=8)
            v_bank[j] = vt_bank
            w_words, w_plane = row_tile_operand(WEIGHTS, h)
            for mt in range(TILES):
                nc.tensor.matmul_mx(
                    out=vt_bank[:, mt, :],
                    lhsT=h_codes[TILES * b + mt].bitcast(FP8X4),
                    lhsT_scale=h_scales[TILES * b + mt],
                    rhs=w_words,
                    rhs_scale=w_plane,
                    start=True,
                    stop=True,
                )

        def bias_v(j):
            if not is_pair(j):
                return
            h = j % HEADS
            nc.vector.tensor_tensor(
                out=v_and_h1(j + 2)[:, 0, :, :],
                in0=v_bank[j][:].rearrange("p t d -> p d t"),
                in1=vb_all[:, h * P : (h + 1) * P].unsqueeze(2).to_broadcast([P, P, PACK]),
                op=ALU.add,
            )

        def attend(j):
            if not is_pair(j):
                return
            for first, count in late_units(j):
                ot_bank = psum.tile([P, count, P], F32, tag="bank", bufs=8)
                o_bank[(j, first)] = ot_bank
                for a in range(count):
                    e_words, e_plane = row_tile_operand(j, first + a)
                    nc.tensor.matmul_mx(
                        out=ot_bank[:, a, :],
                        lhsT=e_words,
                        lhsT_scale=e_plane,
                        rhs=v_codes[j].bitcast(FP8X4),
                        rhs_scale=v_scales[j],
                        start=True,
                        stop=True,
                    )

        def invert_sums(j):
            if not is_pair(j) or j % 2 == 1:
                return
            inv_sums = work.tile([P, 2 * TILES], F32, bufs=3)
            inverse[j // 2] = inv_sums
            nc.vector.reciprocal(out=inv_sums[:], in_=row_sums[j // 2][:])

        def normalise(j):
            if not is_pair(j):
                return
            inv_sum = inverse[j // 2][:, (j % 2) * TILES : (j % 2 + 1) * TILES]
            ot_rows = work.tile([P, TILES, P], F32, bufs=2)
            o_rows[j] = ot_rows
            for first, count in late_units(j):
                by_vector = count - 1 if count == TILES and j % 2 == 1 else count
                nc.vector.tensor_tensor(
                    out=ot_rows[:, first : first + by_vector, :],
                    in0=o_bank[(j, first)][:, 0:by_vector, :],
                    in1=inv_sum[:, first : first + by_vector].unsqueeze(2).to_broadcast([P, by_vector, P]),
                    op=ALU.mult,
                )
                for a in range(by_vector, count):
                    nc.scalar.activation(
                        out=ot_rows[:, first + a, :],
                        in_=o_bank[(j, first)][:, a, :],
                        func=ACT.Copy,
                        scale=inv_sum[:, first + a : first + a + 1],
                    )

        def flip_back(j):
            if not is_pair(j):
                return
            for first, count in late_units(j):
                back_bank = psum.tile([P, count * P], F32, tag="bank", bufs=8)
                o_back[(j, first)] = back_bank
                for a in range(count):
                    nc.tensor.transpose(
                        out=back_bank[:, a * P : (a + 1) * P], in_=o_rows[j][:, first + a, :], identity=ident_f32[:]
                    )

        def finish(j):
            if not is_pair(j):
                return
            b, h = divmod(j, HEADS)
            for first, count in late_units(j):
                y = work.tile([P, count * P], F32, bufs=4)
                nc.scalar.activation(
                    out=y[:],
                    in_=o_back[(j, first)][:],
                    func=ACT.Relu,
                    bias=bn_shift[:, h : h + 1],
                    scale=bn_scale[:, h : h + 1],
                )
                nc.sync.dma_start(out=out[b, h * P : (h + 1) * P, first * P : (first + count) * P], in_=y[:])

        for g in range(TILES):
            group_h1(g)
        for i in range(PAIRS + 3):
            scores(i, 0)
            group_rows(i - 2, 1)
            softmax(i, 0)
            group_h1(i + TILES)

            scores(i, 1)
            bias_v(i - 2)
            invert_sums(i - 2)
            softmax(i, 1)
            if i > 0:
                group_rows(i - 1, 0)

            scores(i, 2)
            flip_back(i - 3)
            quantise_rows(i - 2)
            quantise_v_and_h1(i)
            softmax(i, 2)
            finish(i - 3)

            scores(i, 3)
            if i == 0:
                for nt in range(TILES):
                    flip(WEIGHTS, nt)
                group_rows(WEIGHTS, 0)
            if i == 1:
                quantise_first_h1()
            attend(i - 2)
            project_v(i - 1)
            softmax(i, 3)
            normalise(i - 2)
            if i == 0:
                flip_batch_norm()
            if i == 2:
                fold_batch_norm()
